import numpy as np
import ml_dtypes


def mxq(x, axis, fmt="e4m3"):
    dtype, down = {"e4m3": (ml_dtypes.float8_e4m3fn, 7), "e5m2": (ml_dtypes.float8_e5m2, 14)}[fmt]
    v = np.moveaxis(np.asarray(x, np.float32).astype(ml_dtypes.bfloat16).astype(np.float64), axis, -1)
    blocks = v.reshape(v.shape[:-1] + (-1, 32))
    amax = np.abs(blocks).max(-1, keepdims=True)
    byte = np.maximum(np.where(amax > 0, np.frexp(amax)[1] - 1 + 127, 0) - down, 1)
    scale = np.exp2(byte - 127.0)
    codes = (blocks / scale).astype(np.float32).astype(dtype).astype(np.float64)
    return np.moveaxis((codes * scale).reshape(v.shape), -1, axis)


WIDE = False


def mx_kscale(k):
    if not WIDE:
        return np.ones(k)
    levels = np.array([10, -10, 5, -5, 0])
    if k % 512:
        return np.exp2(np.random.permutation(np.resize(levels, k // 32))).repeat(32)
    a = np.empty((k // 512, 16))
    for p in range(k // 512):
        a[p, :8] = np.random.permutation(np.resize(levels, 8))
        for g in range(8):
            far = levels[np.abs(levels - a[p, g]) >= 10]
            a[p, g + 8] = far[np.random.randint(len(far))]
    return np.exp2(a.ravel()).repeat(32)


BF16 = ml_dtypes.bfloat16


def bf(x):
    return np.asarray(x, np.float32).astype(BF16)


def f64(x):
    return np.asarray(x).astype(np.float64)


B, S, D, E, WINDOW = 8, 512, 1024, 512, 10
HALF = WINDOW // 2


def setup_inputs():
    s, t = mx_kscale(D), mx_kscale(E)
    return {"x": bf(np.random.standard_normal((B, S, D)) * s),
            "Wq": bf(np.random.standard_normal((E, D)) / np.sqrt(D) / s[None, :] * t[:, None]),
            "bq": bf(np.random.standard_normal(E) * 0.1 * t),
            "k": bf(np.random.standard_normal((B, S, E)) / t)}


def reference(x, Wq, bq, k):
    q = (mxq(f64(x), 2, "e4m3") @ mxq(f64(Wq), 1, "e4m3").T) + f64(bq)
    scores = (mxq(q, 2, "e4m3") @ mxq(f64(k), 2, "e4m3").transpose(0, 2, 1)) / np.sqrt(E)
    i = np.arange(S)[:, None]
    j = np.arange(S)[None, :]
    mask = np.abs(i - j) <= HALF
    scores = np.where(mask[None, :, :], scores, -1e9)
    e = np.exp(scores - scores.max(-1, keepdims=True))
    return e / e.sum(-1, keepdims=True)

@@ -1,0 +1,307 @@
+import math
+from contextlib import ExitStack
+
+import concourse.mybir as mybir
+from concourse.masks import make_identity
+
+F32 = mybir.dt.float32
+BF16 = mybir.dt.bfloat16
+U32 = mybir.dt.uint32
+U8 = mybir.dt.uint8
+I32 = mybir.dt.int32
+FP8X4 = mybir.dt.float8_e4m3fn_x4
+ALU = mybir.AluOpType
+ACT = mybir.ActivationFunctionType
+AXIS = mybir.AxisListType
+
+B, S, D, E = 8, 512, 1024, 512
+HALF = 5
+P = 128
+PACK = 4
+K_PASS = P * PACK
+BANK = 512
+BANK_VALUES = 2 * BANK
+R = S // P
+G = D // K_PASS
+W_BANKS = PACK * D // BANK_VALUES
+WIN = P + 2 * HALF
+K_PAD = 64
+N_SCORES = 2 * P
+WIN_START = K_PAD - HALF
+OUT_PAD = 8
+OUT_HOMES = 3
+X_LEAD = 2
+MASKED = -1.0e9
+
+FLOPS = 2 * B * S * D * E + 2 * B * S * S * E
+
+
+def tile_localattention_pa_t_kernel(tc, x, Wq, bq, k, out):
+    nc = tc.nc
+    with ExitStack() as ctx:
+        const = ctx.enter_context(tc.tile_pool(name="const", bufs=1))
+        inputs = ctx.enter_context(tc.tile_pool(name="inputs", bufs=B))
+        work = ctx.enter_context(tc.tile_pool(name="work", bufs=2))
+        psum = ctx.enter_context(tc.psum_pool(name="psum", bufs=8))
+        ctx.enter_context(tc.manual_schedule())
+
+        w_in = const.tile([P, PACK * D], BF16, name="w_in")
+        w_rows = Wq.rearrange("(c t) d -> c t d", t=PACK)
+        for half in range(2):
+            nc.sync.dma_start(
+                out=w_in[:, 2 * D * half : 2 * D * (half + 1)].rearrange("c (t d) -> c t d", t=2),
+                in_=w_rows[:, 2 * half : 2 * half + 2, :],
+            )
+        bias_bf = const.tile([P, PACK], BF16, name="bias_bf")
+        nc.scalar.dma_start(out=bias_bf[:], in_=bq.rearrange("(c t) -> c t", t=PACK))
+        x_in = {}
+        k_in = {}
+
+        def load_x(b):
+            x_in[b] = inputs.tile([P, R * D], BF16, name="x_in")
+            for r in range(R):
+                nc.sync.dma_start(out=x_in[b][:, D * r : D * (r + 1)], in_=x[b, P * r : P * (r + 1), :])
+
+        def load_k(b):
+            k_in[b] = inputs.tile([P, R * E], BF16, name="k_in")
+            nc.sync.dma_start(
+                out=k_in[b][:].rearrange("p (r f) -> p r f", r=R),
+                in_=k[b].rearrange("(r p) f -> p r f", p=P),
+            )
+
+        for b in range(B):
+            load_x(b)
+            load_k(b)
+
+        ident = const.tile([P, P], F32, name="ident")
+        make_identity(nc, ident[:])
+
+        warm = const.tile([P, 1], F32, name="warm")
+        nc.vector.memset(warm[:], 0.0)
+        nc.scalar.activation(out=warm[:], in_=warm[:], func=ACT.Exp)
+
+        mask = const.tile([P, R, WIN], F32, name="mask")
+        nc.gpsimd.memset(mask[:], 0.0)
+        for r in range(R):
+            nc.gpsimd.affine_select(
+                out=mask[:, r, :], in_=mask[:, r, :], pattern=[[1, WIN]],
+                compare_op=ALU.is_ge, fill=MASKED, base=0, channel_multiplier=-1,
+            )
+            nc.gpsimd.affine_select(
+                out=mask[:, r, :], in_=mask[:, r, :], pattern=[[-1, WIN]],
+                compare_op=ALU.is_ge, fill=MASKED, base=2 * HALF, channel_multiplier=1,
+            )
+        nc.gpsimd.memset(mask[:, 0, 0:HALF], MASKED)
+        nc.gpsimd.memset(mask[:, R - 1, WIN - HALF : WIN], MASKED)
+
+        k_codes = []
+        k_scales = []
+        for home in range(2):
+            k_codes.append(const.tile([P, S + 2 * K_PAD], U32, name="k_codes%d" % home, align_bytes=64))
+            k_scales.append(const.tile([P, S + 2 * K_PAD], U8, name="k_scales%d" % home, align_bytes=64))
+            for pad in (slice(0, K_PAD), slice(K_PAD + S, K_PAD + S + K_PAD)):
+                nc.vector.memset(k_codes[home][:, pad].bitcast(I32), 0)
+                nc.vector.memset(k_scales[home][:, pad].bitcast(I32), 0)
+
+        out_tiles = []
+        for home in range(OUT_HOMES):
+            out_tiles.append(const.tile([P, OUT_PAD + R * S + OUT_PAD], F32, name="out_tile%d" % home))
+            nc.vector.memset(out_tiles[home][:], 0.0)
+
+        bias = const.tile([P, PACK], F32, name="bias")
+        nc.vector.tensor_copy(out=bias[:], in_=bias_bf[:])
+
+        def regroup_bank(src, dst, n, copy):
+            src_pairs = src[:].bitcast(F32)
+            dst_pairs = dst[:].bitcast(F32)
+            bank = psum.tile([P, BANK], F32, name="bank")
+            for g in range(2):
+                for u in range(2):
+                    run = BANK * n + 2 * P * g
+                    piece = 2 * g + u
+                    nc.tensor.transpose(
+                        bank[:, P * piece : P * (piece + 1)],
+                        src_pairs[:, run + u : run + 2 * P : 2],
+                        ident[:],
+                    )
+            copy(
+                out=dst_pairs[:, BANK * n : BANK * (n + 1)].rearrange("c (g w u) -> c g w u", g=2, u=2),
+                in_=bank[:].rearrange("c (g u w) -> c g w u", g=2, u=2),
+            )
+
+        def quantise(grouped, codes, scales):
+            nc.vector.quantize_mx(out=codes.bitcast(FP8X4), scales=scales, in_=grouped)
+
+        def quantise_two_banks(grouped, codes, scales, part):
+            values = slice(2 * BANK_VALUES * part, 2 * BANK_VALUES * (part + 1))
+            words = slice(2 * BANK_VALUES // PACK * part, 2 * BANK_VALUES // PACK * (part + 1))
+            quantise(grouped[:, values], codes[:, words], scales[:, words])
+
+        x_grouped = {}
+        x_codes = {}
+        x_scales = {}
+        k_grouped = {}
+        q_grouped = {}
+        q_codes = {}
+        q_scales = {}
+        shifted = {}
+        neg_max = {}
+        expd = {}
+        sums = {}
+        inv_sums = {}
+
+        def new_x(b):
+            x_grouped[b] = work.tile([P, R * D], BF16, name="x_grouped", align_bytes=64)
+
+        def new_x_codes(b):
+            x_codes[b] = work.tile([P, R * G * P], U32, name="x_codes", align_bytes=64)
+            x_scales[b] = work.tile([P, R * G * P], U8, name="x_scales", align_bytes=64)
+
+        def transpose_x(b):
+            new_x(b)
+            for r in range(R):
+                regroup_bank(x_in[b], x_grouped[b], r, nc.scalar.copy)
+
+        def quantise_x(b):
+            new_x_codes(b)
+            for part in range(2):
+                quantise_two_banks(x_grouped[b], x_codes[b], x_scales[b], part)
+
+        def transpose_k(b):
+            k_grouped[b] = work.tile([P, S * PACK], BF16, name="k_grouped", align_bytes=64)
+            for n in range(R // 2):
+                regroup_bank(k_in[b], k_grouped[b], n, nc.scalar.copy)
+
+        def quantise_k(b):
+            quantise(
+                k_grouped[b][:],
+                k_codes[b % 2][:, K_PAD : K_PAD + S],
+                k_scales[b % 2][:, K_PAD : K_PAD + S],
+            )
+
+        def quantise_q(b, part):
+            tokens = slice(2 * P * part, 2 * P * (part + 1))
+            values = slice(2 * P * PACK * part, 2 * P * PACK * (part + 1))
+            quantise(q_grouped[b][:, values], q_codes[b][:, tokens], q_scales[b][:, tokens])
+
+        def project_and_quantise(b):
+            q_grouped[b] = work.tile([P, S * PACK], BF16, name="q_grouped", align_bytes=64)
+            q_codes[b] = work.tile([P, S], U32, name="q_codes", align_bytes=64)
+            q_scales[b] = work.tile([P, S], U8, name="q_scales", align_bytes=64)
+            for r in range(R):
+                bank = psum.tile([P, BANK], F32, name="bank")
+                for t in range(PACK):
+                    for g in range(G):
+                        w_cols = slice(P * (G * t + g), P * (G * t + g + 1))
+                        x_cols = slice(P * (G * r + g), P * (G * r + g + 1))
+                        nc.tensor.matmul_mx(
+                            out=bank[:, P * t : P * (t + 1)],
+                            lhsT=w_codes[:, w_cols].bitcast(FP8X4),
+                            lhsT_scale=w_scales[:, w_cols],
+                            rhs=x_codes[b][:, x_cols].bitcast(FP8X4),
+                            rhs_scale=x_scales[b][:, x_cols],
+                            start=(g == 0),
+                            stop=(g == G - 1),
+                        )
+                nc.vector.tensor_tensor(
+                    out=q_grouped[b][:, BANK * r : BANK * (r + 1)].rearrange("c (w t) -> c w t", t=PACK),
+                    in0=bank[:].rearrange("c (t w) -> c w t", t=PACK),
+                    in1=bias[:].unsqueeze(1).to_broadcast([P, P, PACK]),
+                    op=ALU.add,
+                )
+                if r == R // 2:
+                    quantise_q(b, 0)
+            quantise_k(b)
+            quantise_q(b, 1)
+
+        def scores(b):
+            shifted[b] = work.tile([P, R, WIN], F32, name="shifted")
+            neg_max[b] = work.tile([P, R], F32, name="neg_max")
+            for pair in range(R // 2):
+                bank = psum.tile([P, BANK], F32, name="bank")
+                for side in range(2):
+                    r = 2 * pair + side
+                    nc.tensor.matmul_mx(
+                        out=bank[:, N_SCORES * side : N_SCORES * (side + 1)],
+                        lhsT=q_codes[b][:, P * r : P * (r + 1)].bitcast(FP8X4),
+                        lhsT_scale=q_scales[b][:, P * r : P * (r + 1)],
+                        rhs=k_codes[b % 2][:, P * r : P * r + N_SCORES].bitcast(FP8X4),
+                        rhs_scale=k_scales[b % 2][:, P * r : P * r + N_SCORES],
+                        start=True,
+                        stop=True,
+                    )
+                nc.vector.scalar_tensor_tensor(
+                    out=shifted[b][:, 2 * pair : 2 * pair + 2, :],
+                    in0=bank[:].rearrange("p (side v) -> p side v", side=2)[:, :, WIN_START : WIN_START + WIN],
+                    scalar=1.0 / math.sqrt(E),
+                    in1=mask[:, 2 * pair : 2 * pair + 2, :],
+                    op0=ALU.mult,
+                    op1=ALU.add,
+                )
+            for pair in range(R // 2):
+                nc.vector.tensor_reduce(
+                    out=neg_max[b][:, 2 * pair : 2 * pair + 2], in_=shifted[b][:, 2 * pair : 2 * pair + 2, :],
+                    axis=AXIS.X, op=ALU.max, negate=True,
+                )
+
+        def exponentials(b):
+            expd[b] = work.tile([P, R, WIN], F32, name="expd")
+            sums[b] = work.tile([P, R], F32, name="sums")
+            for r in range(R):
+                nc.scalar.activation(
+                    out=expd[b][:, r, :], in_=shifted[b][:, r, :], func=ACT.Exp,
+                    bias=neg_max[b][:, r : r + 1], scale=1.0, accum_out=sums[b][:, r : r + 1],
+                )
+
+        def invert_sums(b):
+            inv_sums[b] = work.tile([P, R], F32, name="inv_sums")
+            nc.vector.reciprocal(out=inv_sums[b][:], in_=sums[b][:])
+
+        def normalise_and_store(b):
+            for r in range(R):
+                row = OUT_PAD + S * r
+                band = row + P * r - HALF
+                nc.scalar.activation(
+                    out=out_tiles[b % OUT_HOMES][:, band : band + WIN], in_=expd[b][:, r, :], func=ACT.Copy,
+                    scale=inv_sums[b][:, r : r + 1],
+                )
+                nc.sync.dma_start(
+                    out=out[b, P * r : P * (r + 1), :], in_=out_tiles[b % OUT_HOMES][:, row : row + S]
+                )
+
+        w_grouped = const.tile([P, PACK * D], BF16, name="w_grouped", align_bytes=64)
+        w_codes = const.tile([P, PACK * G * P], U32, name="w_codes", align_bytes=64)
+        w_scales = const.tile([P, PACK * G * P], U8, name="w_scales", align_bytes=64)
+        new_x(0)
+        new_x_codes(0)
+        head_copies = (nc.vector.tensor_copy, nc.scalar.copy)
+        for src, grouped, codes, scales in (
+            (w_in, w_grouped, w_codes, w_scales),
+            (x_in[0], x_grouped[0], x_codes[0], x_scales[0]),
+        ):
+            for n in range(W_BANKS):
+                regroup_bank(src, grouped, n, head_copies[n % 2])
+                if n % 2 == 1:
+                    quantise_two_banks(grouped, codes, scales, n // 2)
+        transpose_k(0)
+        project_and_quantise(0)
+
+        x_transposed = 1
+        for i in range(B):
+            if i >= 1:
+                invert_sums(i - 1)
+            x_wanted = min(i + 1 + min(i + 1, X_LEAD), B)
+            for b in range(x_transposed, x_wanted):
+                transpose_x(b)
+            x_transposed = x_wanted
+            if i + 1 < B:
+                transpose_k(i + 1)
+                quantise_x(i + 1)
+            scores(i)
+            if i >= 1:
+                normalise_and_store(i - 1)
+            exponentials(i)
+            if i + 1 < B:
+                project_and_quantise(i + 1)
+        invert_sums(B - 1)
+        normalise_and_store(B - 1)

@@ -20,17 +20,15 @@ P = 128
 PACK = 4
 K_PASS = P * PACK
 BANK = 512
-BANK_VALUES = 2 * BANK
 R = S // P
 G = D // K_PASS
-W_BANKS = PACK * D // BANK_VALUES
+HALF_TILES = 2
 WIN = P + 2 * HALF
 K_PAD = 64
 N_SCORES = 2 * P
 WIN_START = K_PAD - HALF
 OUT_PAD = 8
 OUT_HOMES = 3
-X_LEAD = 2
 MASKED = -1.0e9
 
 FLOPS = 2 * B * S * D * E + 2 * B * S * S * E
@@ -41,7 +39,7 @@ def tile_localattention_pa_t_kernel(tc, x, Wq, bq, k, out):
     with ExitStack() as ctx:
         const = ctx.enter_context(tc.tile_pool(name="const", bufs=1))
         inputs = ctx.enter_context(tc.tile_pool(name="inputs", bufs=B))
-        work = ctx.enter_context(tc.tile_pool(name="work", bufs=2))
+        work = ctx.enter_context(tc.tile_pool(name="work", bufs=3))
         psum = ctx.enter_context(tc.psum_pool(name="psum", bufs=8))
         ctx.enter_context(tc.manual_schedule())
 
@@ -111,13 +109,13 @@ def tile_localattention_pa_t_kernel(tc, x, Wq, bq, k, out):
         bias = const.tile([P, PACK], F32, name="bias")
         nc.vector.tensor_copy(out=bias[:], in_=bias_bf[:])
 
-        def regroup_bank(src, dst, n, copy):
+        def regroup_bank(src, src_bank, dst, dst_bank, copy):
             src_pairs = src[:].bitcast(F32)
             dst_pairs = dst[:].bitcast(F32)
             bank = psum.tile([P, BANK], F32, name="bank")
             for g in range(2):
                 for u in range(2):
-                    run = BANK * n + 2 * P * g
+                    run = BANK * src_bank + 2 * P * g
                     piece = 2 * g + u
                     nc.tensor.transpose(
                         bank[:, P * piece : P * (piece + 1)],
@@ -125,17 +123,14 @@ def tile_localattention_pa_t_kernel(tc, x, Wq, bq, k, out):
                         ident[:],
                     )
             copy(
-                out=dst_pairs[:, BANK * n : BANK * (n + 1)].rearrange("c (g w u) -> c g w u", g=2, u=2),
+                out=dst_pairs[:, BANK * dst_bank : BANK * (dst_bank + 1)].rearrange(
+                    "c (g w u) -> c g w u", g=2, u=2
+                ),
                 in_=bank[:].rearrange("c (g u w) -> c g w u", g=2, u=2),
             )
 
         def quantise(grouped, codes, scales):
             nc.vector.quantize_mx(out=codes.bitcast(FP8X4), scales=scales, in_=grouped)
-
-        def quantise_two_banks(grouped, codes, scales, part):
-            values = slice(2 * BANK_VALUES * part, 2 * BANK_VALUES * (part + 1))
-            words = slice(2 * BANK_VALUES // PACK * part, 2 * BANK_VALUES // PACK * (part + 1))
-            quantise(grouped[:, values], codes[:, words], scales[:, words])
 
         x_grouped = {}
         x_codes = {}
@@ -150,120 +145,107 @@ def tile_localattention_pa_t_kernel(tc, x, Wq, bq, k, out):
         sums = {}
         inv_sums = {}
 
-        def new_x(b):
-            x_grouped[b] = work.tile([P, R * D], BF16, name="x_grouped", align_bytes=64)
+        def transpose_x(n):
+            x_grouped[n] = work.tile([P, HALF_TILES * D], BF16, name="x_grouped", align_bytes=64)
+            for side in range(HALF_TILES):
+                regroup_bank(x_in[n // 2], HALF_TILES * (n % 2) + side, x_grouped[n], side, nc.scalar.copy)
 
-        def new_x_codes(b):
-            x_codes[b] = work.tile([P, R * G * P], U32, name="x_codes", align_bytes=64)
-            x_scales[b] = work.tile([P, R * G * P], U8, name="x_scales", align_bytes=64)
+        def quantise_x(n):
+            x_codes[n] = work.tile([P, HALF_TILES * G * P], U32, name="x_codes", align_bytes=64)
+            x_scales[n] = work.tile([P, HALF_TILES * G * P], U8, name="x_scales", align_bytes=64)
+            quantise(x_grouped[n][:], x_codes[n][:], x_scales[n][:])
 
-        def transpose_x(b):
-            new_x(b)
-            for r in range(R):
-                regroup_bank(x_in[b], x_grouped[b], r, nc.scalar.copy)
+        def transpose_k(n):
+            k_grouped[n] = work.tile([P, HALF_TILES * P * PACK], BF16, name="k_grouped", align_bytes=64)
+            regroup_bank(k_in[n // 2], n % 2, k_grouped[n], 0, nc.scalar.copy)
 
-        def quantise_x(b):
-            new_x_codes(b)
-            for part in range(2):
-                quantise_two_banks(x_grouped[b], x_codes[b], x_scales[b], part)
+        def quantise_k(n):
+            tokens = slice(K_PAD + HALF_TILES * P * (n % 2), K_PAD + HALF_TILES * P * (n % 2 + 1))
+            home = n // 2 % 2
+            quantise(k_grouped[n][:], k_codes[home][:, tokens], k_scales[home][:, tokens])
 
-        def transpose_k(b):
-            k_grouped[b] = work.tile([P, S * PACK], BF16, name="k_grouped", align_bytes=64)
-            for n in range(R // 2):
-                regroup_bank(k_in[b], k_grouped[b], n, nc.scalar.copy)
-
-        def quantise_k(b):
-            quantise(
-                k_grouped[b][:],
-                k_codes[b % 2][:, K_PAD : K_PAD + S],
-                k_scales[b % 2][:, K_PAD : K_PAD + S],
+        def project_tile(n, side):
+            if side == 0:
+                q_grouped[n] = work.tile([P, HALF_TILES * P * PACK], BF16, name="q_grouped", align_bytes=64)
+            bank = psum.tile([P, BANK], F32, name="bank")
+            for t in range(PACK):
+                for g in range(G):
+                    w_cols = slice(P * (G * t + g), P * (G * t + g + 1))
+                    x_cols = slice(P * (G * side + g), P * (G * side + g + 1))
+                    nc.tensor.matmul_mx(
+                        out=bank[:, P * t : P * (t + 1)],
+                        lhsT=w_codes[:, w_cols].bitcast(FP8X4),
+                        lhsT_scale=w_scales[:, w_cols],
+                        rhs=x_codes[n][:, x_cols].bitcast(FP8X4),
+                        rhs_scale=x_scales[n][:, x_cols],
+                        start=(g == 0),
+                        stop=(g == G - 1),
+                    )
+            nc.vector.tensor_tensor(
+                out=q_grouped[n][:, BANK * side : BANK * (side + 1)].rearrange("c (w t) -> c w t", t=PACK),
+                in0=bank[:].rearrange("c (t w) -> c w t", t=PACK),
+                in1=bias[:].unsqueeze(1).to_broadcast([P, P, PACK]),
+                op=ALU.add,
             )
 
-        def quantise_q(b, part):
-            tokens = slice(2 * P * part, 2 * P * (part + 1))
-            values = slice(2 * P * PACK * part, 2 * P * PACK * (part + 1))
-            quantise(q_grouped[b][:, values], q_codes[b][:, tokens], q_scales[b][:, tokens])
+        def quantise_q(n):
+            q_codes[n] = work.tile([P, HALF_TILES * P], U32, name="q_codes", align_bytes=64)
+            q_scales[n] = work.tile([P, HALF_TILES * P], U8, name="q_scales", align_bytes=64)
+            quantise(q_grouped[n][:], q_codes[n][:], q_scales[n][:])
 
-        def project_and_quantise(b):
-            q_grouped[b] = work.tile([P, S * PACK], BF16, name="q_grouped", align_bytes=64)
-            q_codes[b] = work.tile([P, S], U32, name="q_codes", align_bytes=64)
-            q_scales[b] = work.tile([P, S], U8, name="q_scales", align_bytes=64)
-            for r in range(R):
-                bank = psum.tile([P, BANK], F32, name="bank")
-                for t in range(PACK):
-                    for g in range(G):
-                        w_cols = slice(P * (G * t + g), P * (G * t + g + 1))
-                        x_cols = slice(P * (G * r + g), P * (G * r + g + 1))
-                        nc.tensor.matmul_mx(
-                            out=bank[:, P * t : P * (t + 1)],
-                            lhsT=w_codes[:, w_cols].bitcast(FP8X4),
-                            lhsT_scale=w_scales[:, w_cols],
-                            rhs=x_codes[b][:, x_cols].bitcast(FP8X4),
-                            rhs_scale=x_scales[b][:, x_cols],
-                            start=(g == 0),
-                            stop=(g == G - 1),
-                        )
-                nc.vector.tensor_tensor(
-                    out=q_grouped[b][:, BANK * r : BANK * (r + 1)].rearrange("c (w t) -> c w t", t=PACK),
-                    in0=bank[:].rearrange("c (t w) -> c w t", t=PACK),
-                    in1=bias[:].unsqueeze(1).to_broadcast([P, P, PACK]),
-                    op=ALU.add,
+        def scores(n):
+            shifted[n] = work.tile([P, HALF_TILES, WIN], F32, name="shifted")
+            home = n // 2 % 2
+            first = HALF_TILES * (n % 2)
+            bank = psum.tile([P, BANK], F32, name="bank")
+            for side in range(HALF_TILES):
+                k_cols = slice(P * (first + side), P * (first + side) + N_SCORES)
+                nc.tensor.matmul_mx(
+                    out=bank[:, N_SCORES * side : N_SCORES * (side + 1)],
+                    lhsT=q_codes[n][:, P * side : P * (side + 1)].bitcast(FP8X4),
+                    lhsT_scale=q_scales[n][:, P * side : P * (side + 1)],
+                    rhs=k_codes[home][:, k_cols].bitcast(FP8X4),
+                    rhs_scale=k_scales[home][:, k_cols],
+                    start=True,
+                    stop=True,
                 )
-                if r == R // 2:
-                    quantise_q(b, 0)
-            quantise_k(b)
-            quantise_q(b, 1)
+            nc.vector.scalar_tensor_tensor(
+                out=shifted[n][:],
+                in0=bank[:].rearrange("p (side v) -> p side v", side=HALF_TILES)[:, :, WIN_START : WIN_START + WIN],
+                scalar=1.0 / math.sqrt(E),
+                in1=mask[:, first : first + HALF_TILES, :],
+                op0=ALU.mult,
+                op1=ALU.add,
+            )
 
-        def scores(b):
-            shifted[b] = work.tile([P, R, WIN], F32, name="shifted")
-            neg_max[b] = work.tile([P, R], F32, name="neg_max")
-            for pair in range(R // 2):
-                bank = psum.tile([P, BANK], F32, name="bank")
-                for side in range(2):
-                    r = 2 * pair + side
-                    nc.tensor.matmul_mx(
-                        out=bank[:, N_SCORES * side : N_SCORES * (side + 1)],
-                        lhsT=q_codes[b][:, P * r : P * (r + 1)].bitcast(FP8X4),
-                        lhsT_scale=q_scales[b][:, P * r : P * (r + 1)],
-                        rhs=k_codes[b % 2][:, P * r : P * r + N_SCORES].bitcast(FP8X4),
-                        rhs_scale=k_scales[b % 2][:, P * r : P * r + N_SCORES],
-                        start=True,
-                        stop=True,
-                    )
-                nc.vector.scalar_tensor_tensor(
-                    out=shifted[b][:, 2 * pair : 2 * pair + 2, :],
-                    in0=bank[:].rearrange("p (side v) -> p side v", side=2)[:, :, WIN_START : WIN_START + WIN],
-                    scalar=1.0 / math.sqrt(E),
-                    in1=mask[:, 2 * pair : 2 * pair + 2, :],
-                    op0=ALU.mult,
-                    op1=ALU.add,
-                )
-            for pair in range(R // 2):
-                nc.vector.tensor_reduce(
-                    out=neg_max[b][:, 2 * pair : 2 * pair + 2], in_=shifted[b][:, 2 * pair : 2 * pair + 2, :],
-                    axis=AXIS.X, op=ALU.max, negate=True,
-                )
+        def row_maxima(n):
+            neg_max[n] = work.tile([P, HALF_TILES], F32, name="neg_max")
+            nc.vector.tensor_reduce(
+                out=neg_max[n][:], in_=shifted[n][:], axis=AXIS.X, op=ALU.max, negate=True
+            )
 
-        def exponentials(b):
-            expd[b] = work.tile([P, R, WIN], F32, name="expd")
-            sums[b] = work.tile([P, R], F32, name="sums")
-            for r in range(R):
+        def exponentials(n):
+            expd[n] = work.tile([P, HALF_TILES, WIN], F32, name="expd")
+            sums[n] = work.tile([P, HALF_TILES], F32, name="sums")
+            for side in range(HALF_TILES):
                 nc.scalar.activation(
-                    out=expd[b][:, r, :], in_=shifted[b][:, r, :], func=ACT.Exp,
-                    bias=neg_max[b][:, r : r + 1], scale=1.0, accum_out=sums[b][:, r : r + 1],
+                    out=expd[n][:, side, :], in_=shifted[n][:, side, :], func=ACT.Exp,
+                    bias=neg_max[n][:, side : side + 1], scale=1.0, accum_out=sums[n][:, side : side + 1],
                 )
 
-        def invert_sums(b):
-            inv_sums[b] = work.tile([P, R], F32, name="inv_sums")
-            nc.vector.reciprocal(out=inv_sums[b][:], in_=sums[b][:])
+        def invert_sums(n):
+            inv_sums[n] = work.tile([P, HALF_TILES], F32, name="inv_sums")
+            nc.vector.reciprocal(out=inv_sums[n][:], in_=sums[n][:])
 
-        def normalise_and_store(b):
-            for r in range(R):
+        def normalise_and_store(n):
+            b = n // 2
+            for side in range(HALF_TILES):
+                r = HALF_TILES * (n % 2) + side
                 row = OUT_PAD + S * r
                 band = row + P * r - HALF
                 nc.scalar.activation(
-                    out=out_tiles[b % OUT_HOMES][:, band : band + WIN], in_=expd[b][:, r, :], func=ACT.Copy,
-                    scale=inv_sums[b][:, r : r + 1],
+                    out=out_tiles[b % OUT_HOMES][:, band : band + WIN], in_=expd[n][:, side, :], func=ACT.Copy,
+                    scale=inv_sums[n][:, side : side + 1],
                 )
                 nc.sync.dma_start(
                     out=out[b, P * r : P * (r + 1), :], in_=out_tiles[b % OUT_HOMES][:, row : row + S]
@@ -272,36 +254,43 @@ def tile_localattention_pa_t_kernel(tc, x, Wq, bq, k, out):
         w_grouped = const.tile([P, PACK * D], BF16, name="w_grouped", align_bytes=64)
         w_codes = const.tile([P, PACK * G * P], U32, name="w_codes", align_bytes=64)
         w_scales = const.tile([P, PACK * G * P], U8, name="w_scales", align_bytes=64)
-        new_x(0)
-        new_x_codes(0)
-        head_copies = (nc.vector.tensor_copy, nc.scalar.copy)
-        for src, grouped, codes, scales in (
-            (w_in, w_grouped, w_codes, w_scales),
-            (x_in[0], x_grouped[0], x_codes[0], x_scales[0]),
-        ):
-            for n in range(W_BANKS):
-                regroup_bank(src, grouped, n, head_copies[n % 2])
-                if n % 2 == 1:
-                    quantise_two_banks(grouped, codes, scales, n // 2)
-        transpose_k(0)
-        project_and_quantise(0)
+        head_copies = (nc.scalar.copy, nc.vector.tensor_copy)
+        for t in range(PACK):
+            regroup_bank(w_in, t, w_grouped, t, head_copies[t % 2])
+            if t % 2 == 1:
+                half = t // 2
+                values = slice(2 * D * half, 2 * D * (half + 1))
+                words = slice(2 * G * P * half, 2 * G * P * (half + 1))
+                quantise(w_grouped[:, values], w_codes[:, words], w_scales[:, words])
+        transpose_x(0)
+        quantise_x(0)
+        transpose_x(1)
 
-        x_transposed = 1
-        for i in range(B):
-            if i >= 1:
-                invert_sums(i - 1)
-            x_wanted = min(i + 1 + min(i + 1, X_LEAD), B)
-            for b in range(x_transposed, x_wanted):
-                transpose_x(b)
-            x_transposed = x_wanted
-            if i + 1 < B:
-                transpose_k(i + 1)
-                quantise_x(i + 1)
-            scores(i)
-            if i >= 1:
-                normalise_and_store(i - 1)
-            exponentials(i)
-            if i + 1 < B:
-                project_and_quantise(i + 1)
-        invert_sums(B - 1)
-        normalise_and_store(B - 1)
+        halves = 2 * B
+        for n in range(halves + 2):
+            if n + 1 < halves:
+                quantise_x(n + 1)
+            for side in range(HALF_TILES):
+                if n < halves:
+                    project_tile(n, side)
+                if side == 0 and 0 <= n - 2:
+                    invert_sums(n - 2)
+            if 0 <= n - 1 < halves:
+                scores(n - 1)
+            if n < halves:
+                quantise_q(n)
+            if 0 <= n - 1 < halves:
+                row_maxima(n - 1)
+            if 0 <= n - 2:
+                normalise_and_store(n - 2)
+            if n == 0:
+                transpose_k(0)
+                quantise_k(0)
+            if n + 1 < halves:
+                transpose_k(n + 1)
+            if n + 2 < halves:
+                transpose_x(n + 2)
+            if n + 1 < halves:
+                quantise_k(n + 1)
+            if 0 <= n - 1 < halves:
+                exponentials(n - 1)

@@ -45,11 +45,8 @@ def tile_localattention_pa_t_kernel(tc, x, Wq, bq, k, out):
 
         w_in = const.tile([P, PACK * D], BF16, name="w_in")
         w_rows = Wq.rearrange("(c t) d -> c t d", t=PACK)
-        for half in range(2):
-            nc.sync.dma_start(
-                out=w_in[:, 2 * D * half : 2 * D * (half + 1)].rearrange("c (t d) -> c t d", t=2),
-                in_=w_rows[:, 2 * half : 2 * half + 2, :],
-            )
+        for t in range(PACK):
+            nc.sync.dma_start(out=w_in[:, D * t : D * (t + 1)], in_=w_rows[:, t, :])
         bias_bf = const.tile([P, PACK], BF16, name="bias_bf")
         nc.scalar.dma_start(out=bias_bf[:], in_=bq.rearrange("(c t) -> c t", t=PACK))
         x_in = {}
@@ -98,16 +95,15 @@ def tile_localattention_pa_t_kernel(tc, x, Wq, bq, k, out):
             k_codes.append(const.tile([P, S + 2 * K_PAD], U32, name="k_codes%d" % home, align_bytes=64))
             k_scales.append(const.tile([P, S + 2 * K_PAD], U8, name="k_scales%d" % home, align_bytes=64))
             for pad in (slice(0, K_PAD), slice(K_PAD + S, K_PAD + S + K_PAD)):
-                nc.vector.memset(k_codes[home][:, pad].bitcast(I32), 0)
-                nc.vector.memset(k_scales[home][:, pad].bitcast(I32), 0)
+                nc.gpsimd.memset(k_codes[home][:, pad].bitcast(I32), 0)
+                nc.gpsimd.memset(k_scales[home][:, pad].bitcast(I32), 0)
 
         out_tiles = []
         for home in range(OUT_HOMES):
             out_tiles.append(const.tile([P, OUT_PAD + R * S + OUT_PAD], F32, name="out_tile%d" % home))
-            nc.vector.memset(out_tiles[home][:], 0.0)
-
-        bias = const.tile([P, PACK], F32, name="bias")
-        nc.vector.tensor_copy(out=bias[:], in_=bias_bf[:])
+            first = OUT_PAD - HALF + WIN
+            between = out_tiles[home][:, first : first + (R - 1) * (S + P)]
+            nc.vector.memset(between.rearrange("p (gap v) -> p gap v", gap=R - 1)[:, :, 0 : S + P - WIN], 0.0)
 
         def regroup_bank(src, src_bank, dst, dst_bank, copy):
             src_pairs = src[:].bitcast(F32)
@@ -153,7 +149,11 @@ def tile_localattention_pa_t_kernel(tc, x, Wq, bq, k, out):
         def quantise_x(n):
             x_codes[n] = work.tile([P, HALF_TILES * G * P], U32, name="x_codes", align_bytes=64)
             x_scales[n] = work.tile([P, HALF_TILES * G * P], U8, name="x_scales", align_bytes=64)
-            quantise(x_grouped[n][:], x_codes[n][:], x_scales[n][:])
+            parts = HALF_TILES if n == 0 else 1
+            for part in range(parts):
+                values = slice(HALF_TILES * D // parts * part, HALF_TILES * D // parts * (part + 1))
+                words = slice(HALF_TILES * G * P // parts * part, HALF_TILES * G * P // parts * (part + 1))
+                quantise(x_grouped[n][:, values], x_codes[n][:, words], x_scales[n][:, words])
 
         def transpose_k(n):
             k_grouped[n] = work.tile([P, HALF_TILES * P * PACK], BF16, name="k_grouped", align_bytes=64)
@@ -254,42 +254,50 @@ def tile_localattention_pa_t_kernel(tc, x, Wq, bq, k, out):
         w_grouped = const.tile([P, PACK * D], BF16, name="w_grouped", align_bytes=64)
         w_codes = const.tile([P, PACK * G * P], U32, name="w_codes", align_bytes=64)
         w_scales = const.tile([P, PACK * G * P], U8, name="w_scales", align_bytes=64)
-        head_copies = (nc.scalar.copy, nc.vector.tensor_copy)
-        for t in range(PACK):
-            regroup_bank(w_in, t, w_grouped, t, head_copies[t % 2])
-            if t % 2 == 1:
-                half = t // 2
-                values = slice(2 * D * half, 2 * D * (half + 1))
-                words = slice(2 * G * P * half, 2 * G * P * (half + 1))
-                quantise(w_grouped[:, values], w_codes[:, words], w_scales[:, words])
+        def quantise_w(t):
+            words = slice(G * P * t, G * P * (t + 1))
+            quantise(w_grouped[:, D * t : D * (t + 1)], w_codes[:, words], w_scales[:, words])
+
+        regroup_bank(w_in, 0, w_grouped, 0, nc.scalar.copy)
+        regroup_bank(w_in, 1, w_grouped, 1, nc.vector.tensor_copy)
+        quantise_w(0)
+        regroup_bank(w_in, 2, w_grouped, 2, nc.scalar.copy)
+        regroup_bank(w_in, 3, w_grouped, 3, nc.vector.tensor_copy)
+        quantise_w(1)
+        quantise_w(2)
+        quantise_w(3)
         transpose_x(0)
         quantise_x(0)
         transpose_x(1)
+        bias = const.tile([P, PACK], F32, name="bias")
+        nc.vector.tensor_copy(out=bias[:], in_=bias_bf[:])
 
         halves = 2 * B
         for n in range(halves + 2):
+            if n < halves:
+                project_tile(n, 0)
+            if n < halves:
+                project_tile(n, 1)
             if n + 1 < halves:
                 quantise_x(n + 1)
-            for side in range(HALF_TILES):
-                if n < halves:
-                    project_tile(n, side)
-                if side == 0 and 0 <= n - 2:
-                    invert_sums(n - 2)
             if 0 <= n - 1 < halves:
                 scores(n - 1)
             if n < halves:
                 quantise_q(n)
+            if 0 <= n - 2:
+                invert_sums(n - 2)
             if 0 <= n - 1 < halves:
                 row_maxima(n - 1)
-            if 0 <= n - 2:
-                normalise_and_store(n - 2)
             if n == 0:
                 transpose_k(0)
+            if n == 0:
                 quantise_k(0)
             if n + 1 < halves:
                 transpose_k(n + 1)
             if n + 2 < halves:
                 transpose_x(n + 2)
+            if 0 <= n - 2:
+                normalise_and_store(n - 2)
             if n + 1 < halves:
                 quantise_k(n + 1)
             if 0 <= n - 1 < halves:

@@ -102,8 +102,8 @@ def tile_localattention_pa_t_kernel(tc, x, Wq, bq, k, out):
         for home in range(OUT_HOMES):
             out_tiles.append(const.tile([P, OUT_PAD + R * S + OUT_PAD], F32, name="out_tile%d" % home))
             first = OUT_PAD - HALF + WIN
-            between = out_tiles[home][:, first : first + (R - 1) * (S + P)]
-            nc.vector.memset(between.rearrange("p (gap v) -> p gap v", gap=R - 1)[:, :, 0 : S + P - WIN], 0.0)
+            between = out_tiles[home][:].bitcast(I32)[:, first : first + (R - 1) * (S + P)]
+            nc.vector.memset(between.rearrange("p (gap v) -> p gap v", gap=R - 1)[:, :, 0 : S + P - WIN], 0)
 
         def regroup_bank(src, src_bank, dst, dst_bank, copy):
             src_pairs = src[:].bitcast(F32)
@@ -237,19 +237,36 @@ def tile_localattention_pa_t_kernel(tc, x, Wq, bq, k, out):
             inv_sums[n] = work.tile([P, HALF_TILES], F32, name="inv_sums")
             nc.vector.reciprocal(out=inv_sums[n][:], in_=sums[n][:])
 
+        def store(b, r, first, last):
+            row = OUT_PAD + S * r
+            nc.sync.dma_start(
+                out=out[b, P * r : P * (r + 1), first:last],
+                in_=out_tiles[b % OUT_HOMES][:, row + first : row + last],
+            )
+
+        def band_columns(r):
+            return max(P * r - OUT_PAD, 0), min(P * (r + 1) + OUT_PAD, S)
+
+        def store_zeros_of_last_half():
+            for r in range(R - HALF_TILES, R):
+                first, last = band_columns(r)
+                store(B - 1, r, 0, first)
+                if last < S:
+                    store(B - 1, r, last, S)
+
         def normalise_and_store(n):
             b = n // 2
             for side in range(HALF_TILES):
                 r = HALF_TILES * (n % 2) + side
-                row = OUT_PAD + S * r
-                band = row + P * r - HALF
+                band = OUT_PAD + (S + P) * r - HALF
                 nc.scalar.activation(
                     out=out_tiles[b % OUT_HOMES][:, band : band + WIN], in_=expd[n][:, side, :], func=ACT.Copy,
                     scale=inv_sums[n][:, side : side + 1],
                 )
-                nc.sync.dma_start(
-                    out=out[b, P * r : P * (r + 1), :], in_=out_tiles[b % OUT_HOMES][:, row : row + S]
-                )
+                if n == 2 * B - 1:
+                    store(b, r, *band_columns(r))
+                else:
+                    store(b, r, 0, S)
 
         w_grouped = const.tile([P, PACK * D], BF16, name="w_grouped", align_bytes=64)
         w_codes = const.tile([P, PACK * G * P], U32, name="w_codes", align_bytes=64)
@@ -298,6 +315,8 @@ def tile_localattention_pa_t_kernel(tc, x, Wq, bq, k, out):
                 transpose_x(n + 2)
             if 0 <= n - 2:
                 normalise_and_store(n - 2)
+            if n == 2 * B - 7:
+                store_zeros_of_last_half()
             if n + 1 < halves:
                 quantise_k(n + 1)
             if 0 <= n - 1 < halves:

@@ -74,20 +74,23 @@ def tile_localattention_pa_t_kernel(tc, x, Wq, bq, k, out):
         warm = const.tile([P, 1], F32, name="warm")
         nc.vector.memset(warm[:], 0.0)
         nc.scalar.activation(out=warm[:], in_=warm[:], func=ACT.Exp)
+        zero = const.tile([P, 1], F32, name="zero")
+        nc.vector.memset(zero[:], 0.0)
 
+        band = const.tile([P, WIN], F32, name="band")
+        nc.gpsimd.memset(band[:], 0.0)
+        nc.gpsimd.affine_select(
+            out=band[:], in_=band[:], pattern=[[1, WIN]],
+            compare_op=ALU.is_ge, fill=MASKED, base=0, channel_multiplier=-1,
+        )
+        nc.gpsimd.affine_select(
+            out=band[:], in_=band[:], pattern=[[-1, WIN]],
+            compare_op=ALU.is_ge, fill=MASKED, base=2 * HALF, channel_multiplier=1,
+        )
         mask = const.tile([P, R, WIN], F32, name="mask")
-        nc.gpsimd.memset(mask[:], 0.0)
-        for r in range(R):
-            nc.gpsimd.affine_select(
-                out=mask[:, r, :], in_=mask[:, r, :], pattern=[[1, WIN]],
-                compare_op=ALU.is_ge, fill=MASKED, base=0, channel_multiplier=-1,
-            )
-            nc.gpsimd.affine_select(
-                out=mask[:, r, :], in_=mask[:, r, :], pattern=[[-1, WIN]],
-                compare_op=ALU.is_ge, fill=MASKED, base=2 * HALF, channel_multiplier=1,
-            )
-        nc.gpsimd.memset(mask[:, 0, 0:HALF], MASKED)
-        nc.gpsimd.memset(mask[:, R - 1, WIN - HALF : WIN], MASKED)
+        nc.vector.tensor_copy(out=mask[:], in_=band[:].unsqueeze(1).to_broadcast([P, R, WIN]))
+        nc.vector.memset(mask[:, 0, 0:HALF], MASKED)
+        nc.vector.memset(mask[:, R - 1, WIN - HALF : WIN], MASKED)
 
         k_codes = []
         k_scales = []
@@ -101,9 +104,16 @@ def tile_localattention_pa_t_kernel(tc, x, Wq, bq, k, out):
         out_tiles = []
         for home in range(OUT_HOMES):
             out_tiles.append(const.tile([P, OUT_PAD + R * S + OUT_PAD], F32, name="out_tile%d" % home))
+
+        def zero_out_tile(home):
             first = OUT_PAD - HALF + WIN
-            between = out_tiles[home][:].bitcast(I32)[:, first : first + (R - 1) * (S + P)]
-            nc.vector.memset(between.rearrange("p (gap v) -> p gap v", gap=R - 1)[:, :, 0 : S + P - WIN], 0)
+            between = out_tiles[home][:, first : first + (R - 1) * (S + P)]
+            nc.scalar.copy(
+                out=between.rearrange("p (gap v) -> p gap v", gap=R - 1)[:, :, 0 : S + P - WIN],
+                in_=zero[:].unsqueeze(1).to_broadcast([P, R - 1, S + P - WIN]),
+            )
+
+        zero_out_tile(0)
 
         def regroup_bank(src, src_bank, dst, dst_bank, copy):
             src_pairs = src[:].bitcast(F32)
@@ -305,6 +315,8 @@ def tile_localattention_pa_t_kernel(tc, x, Wq, bq, k, out):
                 invert_sums(n - 2)
             if 0 <= n - 1 < halves:
                 row_maxima(n - 1)
+            if n + 1 < OUT_HOMES:
+                zero_out_tile(n + 1)
             if n == 0:
                 transpose_k(0)
             if n == 0:

import math
from contextlib import ExitStack

import concourse.mybir as mybir
from concourse.masks import make_identity

F32 = mybir.dt.float32
BF16 = mybir.dt.bfloat16
U32 = mybir.dt.uint32
U8 = mybir.dt.uint8
I32 = mybir.dt.int32
FP8X4 = mybir.dt.float8_e4m3fn_x4
ALU = mybir.AluOpType
ACT = mybir.ActivationFunctionType
AXIS = mybir.AxisListType

B, S, D, E = 8, 512, 1024, 512
HALF = 5
P = 128
PACK = 4
K_PASS = P * PACK
BANK = 512
R = S // P
G = D // K_PASS
HALF_TILES = 2
WIN = P + 2 * HALF
K_PAD = 64
N_SCORES = 2 * P
WIN_START = K_PAD - HALF
OUT_PAD = 8
OUT_HOMES = 3
MASKED = -1.0e9

FLOPS = 2 * B * S * D * E + 2 * B * S * S * E


def tile_localattention_pa_t_kernel(tc, x, Wq, bq, k, out):
    nc = tc.nc
    with ExitStack() as ctx:
        const = ctx.enter_context(tc.tile_pool(name="const", bufs=1))
        inputs = ctx.enter_context(tc.tile_pool(name="inputs", bufs=B))
        work = ctx.enter_context(tc.tile_pool(name="work", bufs=3))
        psum = ctx.enter_context(tc.psum_pool(name="psum", bufs=8))
        ctx.enter_context(tc.manual_schedule())

        w_in = const.tile([P, PACK * D], BF16, name="w_in")
        w_rows = Wq.rearrange("(c t) d -> c t d", t=PACK)
        for t in range(PACK):
            nc.sync.dma_start(out=w_in[:, D * t : D * (t + 1)], in_=w_rows[:, t, :])
        bias_bf = const.tile([P, PACK], BF16, name="bias_bf")
        nc.scalar.dma_start(out=bias_bf[:], in_=bq.rearrange("(c t) -> c t", t=PACK))
        x_in = {}
        k_in = {}

        def load_x(b):
            x_in[b] = inputs.tile([P, R * D], BF16, name="x_in")
            for r in range(R):
                nc.sync.dma_start(out=x_in[b][:, D * r : D * (r + 1)], in_=x[b, P * r : P * (r + 1), :])

        def load_k(b):
            k_in[b] = inputs.tile([P, R * E], BF16, name="k_in")
            nc.sync.dma_start(
                out=k_in[b][:].rearrange("p (r f) -> p r f", r=R),
                in_=k[b].rearrange("(r p) f -> p r f", p=P),
            )

        for b in range(B):
            load_x(b)
            load_k(b)

        ident = const.tile([P, P], F32, name="ident")
        make_identity(nc, ident[:])

        warm = const.tile([P, 1], F32, name="warm")
        nc.vector.memset(warm[:], 0.0)
        nc.scalar.activation(out=warm[:], in_=warm[:], func=ACT.Exp)
        zero = const.tile([P, 1], F32, name="zero")
        nc.vector.memset(zero[:], 0.0)

        band = const.tile([P, WIN], F32, name="band")
        nc.gpsimd.memset(band[:], 0.0)
        nc.gpsimd.affine_select(
            out=band[:], in_=band[:], pattern=[[1, WIN]],
            compare_op=ALU.is_ge, fill=MASKED, base=0, channel_multiplier=-1,
        )
        nc.gpsimd.affine_select(
            out=band[:], in_=band[:], pattern=[[-1, WIN]],
            compare_op=ALU.is_ge, fill=MASKED, base=2 * HALF, channel_multiplier=1,
        )
        mask = const.tile([P, R, WIN], F32, name="mask")
        nc.vector.tensor_copy(out=mask[:], in_=band[:].unsqueeze(1).to_broadcast([P, R, WIN]))
        nc.vector.memset(mask[:, 0, 0:HALF], MASKED)
        nc.vector.memset(mask[:, R - 1, WIN - HALF : WIN], MASKED)

        k_codes = []
        k_scales = []
        for home in range(2):
            k_codes.append(const.tile([P, S + 2 * K_PAD], U32, name="k_codes%d" % home, align_bytes=64))
            k_scales.append(const.tile([P, S + 2 * K_PAD], U8, name="k_scales%d" % home, align_bytes=64))
            for pad in (slice(0, K_PAD), slice(K_PAD + S, K_PAD + S + K_PAD)):
                nc.gpsimd.memset(k_codes[home][:, pad].bitcast(I32), 0)
                nc.gpsimd.memset(k_scales[home][:, pad].bitcast(I32), 0)

        out_tiles = []
        for home in range(OUT_HOMES):
            out_tiles.append(const.tile([P, OUT_PAD + R * S + OUT_PAD], F32, name="out_tile%d" % home))

        def zero_out_tile(home):
            first = OUT_PAD - HALF + WIN
            between = out_tiles[home][:, first : first + (R - 1) * (S + P)]
            nc.scalar.copy(
                out=between.rearrange("p (gap v) -> p gap v", gap=R - 1)[:, :, 0 : S + P - WIN],
                in_=zero[:].unsqueeze(1).to_broadcast([P, R - 1, S + P - WIN]),
            )

        zero_out_tile(0)

        def regroup_bank(src, src_bank, dst, dst_bank, copy):
            src_pairs = src[:].bitcast(F32)
            dst_pairs = dst[:].bitcast(F32)
            bank = psum.tile([P, BANK], F32, name="bank")
            for g in range(2):
                for u in range(2):
                    run = BANK * src_bank + 2 * P * g
                    piece = 2 * g + u
                    nc.tensor.transpose(
                        bank[:, P * piece : P * (piece + 1)],
                        src_pairs[:, run + u : run + 2 * P : 2],
                        ident[:],
                    )
            copy(
                out=dst_pairs[:, BANK * dst_bank : BANK * (dst_bank + 1)].rearrange(
                    "c (g w u) -> c g w u", g=2, u=2
                ),
                in_=bank[:].rearrange("c (g u w) -> c g w u", g=2, u=2),
            )

        def quantise(grouped, codes, scales):
            nc.vector.quantize_mx(out=codes.bitcast(FP8X4), scales=scales, in_=grouped)

        x_grouped = {}
        x_codes = {}
        x_scales = {}
        k_grouped = {}
        q_grouped = {}
        q_codes = {}
        q_scales = {}
        shifted = {}
        neg_max = {}
        expd = {}
        sums = {}
        inv_sums = {}

        def transpose_x(n):
            x_grouped[n] = work.tile([P, HALF_TILES * D], BF16, name="x_grouped", align_bytes=64)
            for side in range(HALF_TILES):
                regroup_bank(x_in[n // 2], HALF_TILES * (n % 2) + side, x_grouped[n], side, nc.scalar.copy)

        def quantise_x(n):
            x_codes[n] = work.tile([P, HALF_TILES * G * P], U32, name="x_codes", align_bytes=64)
            x_scales[n] = work.tile([P, HALF_TILES * G * P], U8, name="x_scales", align_bytes=64)
            parts = HALF_TILES if n == 0 else 1
            for part in range(parts):
                values = slice(HALF_TILES * D // parts * part, HALF_TILES * D // parts * (part + 1))
                words = slice(HALF_TILES * G * P // parts * part, HALF_TILES * G * P // parts * (part + 1))
                quantise(x_grouped[n][:, values], x_codes[n][:, words], x_scales[n][:, words])

        def transpose_k(n):
            k_grouped[n] = work.tile([P, HALF_TILES * P * PACK], BF16, name="k_grouped", align_bytes=64)
            regroup_bank(k_in[n // 2], n % 2, k_grouped[n], 0, nc.scalar.copy)

        def quantise_k(n):
            tokens = slice(K_PAD + HALF_TILES * P * (n % 2), K_PAD + HALF_TILES * P * (n % 2 + 1))
            home = n // 2 % 2
            quantise(k_grouped[n][:], k_codes[home][:, tokens], k_scales[home][:, tokens])

        def project_tile(n, side):
            if side == 0:
                q_grouped[n] = work.tile([P, HALF_TILES * P * PACK], BF16, name="q_grouped", align_bytes=64)
            bank = psum.tile([P, BANK], F32, name="bank")
            for t in range(PACK):
                for g in range(G):
                    w_cols = slice(P * (G * t + g), P * (G * t + g + 1))
                    x_cols = slice(P * (G * side + g), P * (G * side + g + 1))
                    nc.tensor.matmul_mx(
                        out=bank[:, P * t : P * (t + 1)],
                        lhsT=w_codes[:, w_cols].bitcast(FP8X4),
                        lhsT_scale=w_scales[:, w_cols],
                        rhs=x_codes[n][:, x_cols].bitcast(FP8X4),
                        rhs_scale=x_scales[n][:, x_cols],
                        start=(g == 0),
                        stop=(g == G - 1),
                    )
            nc.vector.tensor_tensor(
                out=q_grouped[n][:, BANK * side : BANK * (side + 1)].rearrange("c (w t) -> c w t", t=PACK),
                in0=bank[:].rearrange("c (t w) -> c w t", t=PACK),
                in1=bias[:].unsqueeze(1).to_broadcast([P, P, PACK]),
                op=ALU.add,
            )

        def quantise_q(n):
            q_codes[n] = work.tile([P, HALF_TILES * P], U32, name="q_codes", align_bytes=64)
            q_scales[n] = work.tile([P, HALF_TILES * P], U8, name="q_scales", align_bytes=64)
            quantise(q_grouped[n][:], q_codes[n][:], q_scales[n][:])

        def scores(n):
            shifted[n] = work.tile([P, HALF_TILES, WIN], F32, name="shifted")
            home = n // 2 % 2
            first = HALF_TILES * (n % 2)
            bank = psum.tile([P, BANK], F32, name="bank")
            for side in range(HALF_TILES):
                k_cols = slice(P * (first + side), P * (first + side) + N_SCORES)
                nc.tensor.matmul_mx(
                    out=bank[:, N_SCORES * side : N_SCORES * (side + 1)],
                    lhsT=q_codes[n][:, P * side : P * (side + 1)].bitcast(FP8X4),
                    lhsT_scale=q_scales[n][:, P * side : P * (side + 1)],
                    rhs=k_codes[home][:, k_cols].bitcast(FP8X4),
                    rhs_scale=k_scales[home][:, k_cols],
                    start=True,
                    stop=True,
                )
            nc.vector.scalar_tensor_tensor(
                out=shifted[n][:],
                in0=bank[:].rearrange("p (side v) -> p side v", side=HALF_TILES)[:, :, WIN_START : WIN_START + WIN],
                scalar=1.0 / math.sqrt(E),
                in1=mask[:, first : first + HALF_TILES, :],
                op0=ALU.mult,
                op1=ALU.add,
            )

        def row_maxima(n):
            neg_max[n] = work.tile([P, HALF_TILES], F32, name="neg_max")
            nc.vector.tensor_reduce(
                out=neg_max[n][:], in_=shifted[n][:], axis=AXIS.X, op=ALU.max, negate=True
            )

        def exponentials(n):
            expd[n] = work.tile([P, HALF_TILES, WIN], F32, name="expd")
            sums[n] = work.tile([P, HALF_TILES], F32, name="sums")
            for side in range(HALF_TILES):
                nc.scalar.activation(
                    out=expd[n][:, side, :], in_=shifted[n][:, side, :], func=ACT.Exp,
                    bias=neg_max[n][:, side : side + 1], scale=1.0, accum_out=sums[n][:, side : side + 1],
                )

        def invert_sums(n):
            inv_sums[n] = work.tile([P, HALF_TILES], F32, name="inv_sums")
            nc.vector.reciprocal(out=inv_sums[n][:], in_=sums[n][:])

        def store(b, r, first, last):
            row = OUT_PAD + S * r
            nc.sync.dma_start(
                out=out[b, P * r : P * (r + 1), first:last],
                in_=out_tiles[b % OUT_HOMES][:, row + first : row + last],
            )

        def band_columns(r):
            return max(P * r - OUT_PAD, 0), min(P * (r + 1) + OUT_PAD, S)

        def store_zeros_of_last_half():
            for r in range(R - HALF_TILES, R):
                first, last = band_columns(r)
                store(B - 1, r, 0, first)
                if last < S:
                    store(B - 1, r, last, S)

        def normalise_and_store(n):
            b = n // 2
            for side in range(HALF_TILES):
                r = HALF_TILES * (n % 2) + side
                band = OUT_PAD + (S + P) * r - HALF
                nc.scalar.activation(
                    out=out_tiles[b % OUT_HOMES][:, band : band + WIN], in_=expd[n][:, side, :], func=ACT.Copy,
                    scale=inv_sums[n][:, side : side + 1],
                )
                if n == 2 * B - 1:
                    store(b, r, *band_columns(r))
                else:
                    store(b, r, 0, S)

        w_grouped = const.tile([P, PACK * D], BF16, name="w_grouped", align_bytes=64)
        w_codes = const.tile([P, PACK * G * P], U32, name="w_codes", align_bytes=64)
        w_scales = const.tile([P, PACK * G * P], U8, name="w_scales", align_bytes=64)
        def quantise_w(t):
            words = slice(G * P * t, G * P * (t + 1))
            quantise(w_grouped[:, D * t : D * (t + 1)], w_codes[:, words], w_scales[:, words])

        regroup_bank(w_in, 0, w_grouped, 0, nc.scalar.copy)
        regroup_bank(w_in, 1, w_grouped, 1, nc.vector.tensor_copy)
        quantise_w(0)
        regroup_bank(w_in, 2, w_grouped, 2, nc.scalar.copy)
        regroup_bank(w_in, 3, w_grouped, 3, nc.vector.tensor_copy)
        quantise_w(1)
        quantise_w(2)
        quantise_w(3)
        transpose_x(0)
        quantise_x(0)
        transpose_x(1)
        bias = const.tile([P, PACK], F32, name="bias")
        nc.vector.tensor_copy(out=bias[:], in_=bias_bf[:])

        halves = 2 * B
        for n in range(halves + 2):
            if n < halves:
                project_tile(n, 0)
            if n < halves:
                project_tile(n, 1)
            if n + 1 < halves:
                quantise_x(n + 1)
            if 0 <= n - 1 < halves:
                scores(n - 1)
            if n < halves:
                quantise_q(n)
            if 0 <= n - 2:
                invert_sums(n - 2)
            if 0 <= n - 1 < halves:
                row_maxima(n - 1)
            if n + 1 < OUT_HOMES:
                zero_out_tile(n + 1)
            if n == 0:
                transpose_k(0)
            if n == 0:
                quantise_k(0)
            if n + 1 < halves:
                transpose_k(n + 1)
            if n + 2 < halves:
                transpose_x(n + 2)
            if 0 <= n - 2:
                normalise_and_store(n - 2)
            if n == 2 * B - 7:
                store_zeros_of_last_half()
            if n + 1 < halves:
                quantise_k(n + 1)
            if 0 <= n - 1 < halves:
                exponentials(n - 1)
